import numpy as np
import ml_dtypes


def mxq(x, axis, fmt="e4m3"):
    dtype, down = {"e4m3": (ml_dtypes.float8_e4m3fn, 7), "e5m2": (ml_dtypes.float8_e5m2, 14)}[fmt]
    v = np.moveaxis(np.asarray(x, np.float32).astype(ml_dtypes.bfloat16).astype(np.float64), axis, -1)
    blocks = v.reshape(v.shape[:-1] + (-1, 32))
    amax = np.abs(blocks).max(-1, keepdims=True)
    byte = np.maximum(np.where(amax > 0, np.frexp(amax)[1] - 1 + 127, 0) - down, 1)
    scale = np.exp2(byte - 127.0)
    codes = (blocks / scale).astype(np.float32).astype(dtype).astype(np.float64)
    return np.moveaxis((codes * scale).reshape(v.shape), -1, axis)


WIDE = False


def mx_kscale(k):
    if not WIDE:
        return np.ones(k)
    levels = np.array([10, -10, 5, -5, 0])
    a = np.random.permutation(np.resize(levels, k // 512 * 4)).reshape(k // 512, 4)
    idx = np.arange(k)
    return np.exp2(a[idx // 512, idx % 128 // 32])


BF16 = ml_dtypes.bfloat16


def bf(x):
    return np.asarray(x, np.float32).astype(BF16)


def f64(x):
    return np.asarray(x).astype(np.float64)


E2M1 = np.array([0.0, 0.5, 1.0, 1.5, 2.0, 3.0, 4.0, 6.0, -0.0, -0.5, -1.0, -1.5, -2.0, -3.0, -4.0, -6.0])


def pack_weight(w, fmt):
    k, n = w.shape
    w = f64(bf(w)).reshape(k // 32, 32, n)
    amax = np.abs(w).max(1)
    if fmt == "e4m3":
        byte = np.frexp(amax)[1] - 1 + 127 - 7
    else:
        mant, ex = np.frexp(amax / 6.0)
        byte = np.where(mant > 0.5, ex, ex - 1) + 127
    byte = np.clip(np.where(amax > 0, byte, 1), 1, 254)
    scaled = (w * np.exp2(127.0 - byte)[:, None, :]).reshape(k, n).astype(np.float32)
    by_word = np.ascontiguousarray(scaled.reshape(k // 512, 128, 4, n).transpose(0, 1, 3, 2))
    if fmt == "e4m3":
        words = by_word.astype(ml_dtypes.float8_e4m3fn).view(np.uint8)
    else:
        c = by_word.astype(ml_dtypes.float4_e2m1fn).view(np.uint8) & 0xF
        words = c[..., 0::2] | (c[..., 1::2] << 4)
    return np.ascontiguousarray(words), np.ascontiguousarray(byte.astype(np.uint8).reshape(k // 512, 16, n))


def unpack_weight(words, scales, fmt):
    g, p, n, _ = words.shape
    if fmt == "e4m3":
        vals = np.ascontiguousarray(words).view(ml_dtypes.float8_e4m3fn).astype(np.float64)
    else:
        nib = np.empty((g, p, n, 4), np.uint8)
        nib[..., 0::2] = words & 0xF
        nib[..., 1::2] = words >> 4
        vals = E2M1[nib]
    vals = vals * np.repeat(np.exp2(scales.astype(np.float64) - 127.0), 8, axis=1)[..., None]
    return vals.transpose(0, 1, 3, 2).reshape(g * 512, n)


B, T, D, F, KC = 1, 128, 2048, 4096, 4


def silu(v):
    return v / (1.0 + np.exp(-v))


def causal_dconv1d(x, w, residual=True):
    n_t = x.shape[1]
    k_size = w.shape[1]
    xp = np.pad(x, ((0, 0), (k_size - 1, 0), (0, 0)))
    out = xp[:, 0:n_t, :] * w[:, 0]
    for k in range(1, k_size):
        out = out + xp[:, k:k + n_t, :] * w[:, k]
    return x + out if residual else out


def setup_inputs():
    s, t = mx_kscale(D), mx_kscale(F)
    x = bf(np.random.standard_normal((B, T, D)) * s)
    w_gate_words, w_gate_scales = pack_weight((np.random.standard_normal((F, D)) / np.sqrt(D) / s[None, :]).T, "e4m3")
    w_up_words, w_up_scales = pack_weight((np.random.standard_normal((F, D)) / np.sqrt(D) / s[None, :] * t[:, None]).T, "e4m3")
    w_down_words, w_down_scales = pack_weight((np.random.standard_normal((D, F)) / np.sqrt(F) / t[None, :]).T, "e4m3")
    conv_w = bf(np.random.standard_normal((2 * F, KC)) * 0.2)
    return {"x": x,
            "w_gate_words": w_gate_words, "w_gate_scales": w_gate_scales,
            "w_up_words": w_up_words, "w_up_scales": w_up_scales,
            "w_down_words": w_down_words, "w_down_scales": w_down_scales,
            "conv_w": conv_w}


def reference(x, w_gate_words, w_gate_scales, w_up_words, w_up_scales, w_down_words, w_down_scales, conv_w):
    xq = mxq(f64(x), 2, "e4m3")
    gate = xq @ unpack_weight(w_gate_words, w_gate_scales, "e4m3")
    up = xq @ unpack_weight(w_up_words, w_up_scales, "e4m3")
    d_ff = w_gate_words.shape[2]
    cw = f64(conv_w)
    gate = causal_dconv1d(gate, cw[:d_ff], residual=True)
    up = causal_dconv1d(up, cw[d_ff:], residual=True)
    h = up * silu(gate)
    return mxq(h, 2, "e4m3") @ unpack_weight(w_down_words, w_down_scales, "e4m3")

@@ -1,0 +1,272 @@
+from contextlib import ExitStack
+
+import concourse.mybir as mybir
+from concourse.masks import make_identity
+
+F32 = mybir.dt.float32
+BF16 = mybir.dt.bfloat16
+I32 = mybir.dt.int32
+U32 = mybir.dt.uint32
+U8 = mybir.dt.uint8
+FP8X4 = mybir.dt.float8_e4m3fn_x4
+ALU = mybir.AluOpType
+ACT = mybir.ActivationFunctionType
+
+P = 128
+T = 128
+D = 2048
+F = 4096
+KP = 512
+GD = D // KP
+GF = F // KP
+UNIT = 1024
+NUNIT = F // UNIT
+RING = 6
+FLOPS = 3 * 2 * T * D * F
+
+
+def tile_canonglufeedforwardlayer_w_kernel(tc, x, wg_w, wg_s, wu_w, wu_s, wd_w, wd_s, conv_w, out):
+    nc = tc.nc
+    with ExitStack() as ctx:
+        ctx.enter_context(tc.manual_schedule())
+        const = ctx.enter_context(tc.tile_pool(name="const", bufs=1))
+        wpool = ctx.enter_context(tc.tile_pool(name="wpool", bufs=RING))
+        work = ctx.enter_context(tc.tile_pool(name="work", bufs=2))
+        psum = ctx.enter_context(tc.psum_pool(name="psum", bufs=1))
+
+        gpl = const.tile([P, F], U8, name="gpl", align_bytes=64)
+        upl = const.tile([P, F], U8, name="upl", align_bytes=64)
+        dpl = const.tile([P, 2, D], U8, name="dpl", align_bytes=64)
+        cw_sb = const.tile([P, 4 * P], BF16, name="cw_sb")
+        warm = const.tile([P, 8], F32, name="warm")
+        nc.vector.memset(cw_sb[:].bitcast(I32), 0)
+        nc.vector.memset(gpl[:].bitcast(I32), 0)
+        nc.vector.memset(upl[:].bitcast(I32), 0)
+        nc.vector.memset(warm[:], 0.0)
+        nc.vector.memset(dpl[:].rearrange("p h n -> p (h n)").bitcast(I32), 0)
+
+        x_sb = const.tile([P, D], BF16, name="x_sb")
+        nc.sync.dma_start(out=x_sb[:], in_=x.rearrange("b t d -> (b t) d"))
+        nc.scalar.dma_start(out=cw_sb[0:64, :], in_=conv_w.rearrange("(a m) k -> a (m k)", m=P))
+        nc.scalar.activation(out=warm[:, 4:8], in_=warm[:, 0:4], func=ACT.Silu)
+        for pl, sc in ((gpl, wg_s), (upl, wu_s)):
+            for q in range(4):
+                nc.sync.dma_start(
+                    out=pl[32 * q : 32 * q + 16, :].bitcast(I32),
+                    in_=sc[:, 4 * q : 4 * q + 4, :].bitcast(I32),
+                )
+
+        wviews = (
+            wg_w.rearrange("g p n t -> p g (n t)").bitcast(I32),
+            wu_w.rearrange("g p n t -> p g (n t)").bitcast(I32),
+        )
+        units = {}
+
+        def load_unit(i):
+            c, br = divmod(i, 2)
+            wt = wpool.tile([P, GD, UNIT], U32, name="wt", align_bytes=64)
+            nc.sync.dma_start(out=wt[:].bitcast(I32), in_=wviews[br][:, :, UNIT * c : UNIT * (c + 1)])
+            units[(c, br)] = wt
+
+        dws = {}
+
+        def load_down():
+            for h in range(2):
+                for q in range(4):
+                    nc.sync.dma_start(
+                        out=dpl[32 * q : 32 * q + 16, h, :].bitcast(I32),
+                        in_=wd_s[4 * h : 4 * h + 4, 4 * q : 4 * q + 4, :].bitcast(I32),
+                    )
+            for b in range(GF):
+                src = wd_w[b].rearrange("p n t -> p (n t)").bitcast(I32)
+                parts = 2 if b == GF - 1 else 1
+                w = D // parts
+                for i in range(parts):
+                    dw = const.tile([P, w], U32, name="dw%d_%d" % (b, i), align_bytes=64)
+                    nc.sync.dma_start(out=dw[:].bitcast(I32), in_=src[:, w * i : w * (i + 1)])
+                    for n in range(w * i // KP, w * (i + 1) // KP):
+                        dws[(b, n)] = dw[:, KP * n - w * i : KP * (n + 1) - w * i]
+
+        for i in range(RING):
+            load_unit(i)
+
+        identf = const.tile([P, P], F32, name="identf")
+        make_identity(nc, identf[:])
+        sel = const.tile([P, 4, 4, P], BF16, name="sel")
+        nc.gpsimd.memset(sel[:].rearrange("m j a p -> m (j a p)").bitcast(F32), 0.0)
+        for a in range(4):
+            nc.gpsimd.tensor_copy(
+                out=sel[:, :, a, 32 * a : 32 * a + 32],
+                in_=identf[:].rearrange("m (q j) -> m j q", j=4),
+            )
+
+        cwf = const.tile([P, 4, P], F32, name="cwf")
+        nc.vector.tensor_copy(out=cwf[:], in_=cw_sb[:].rearrange("a (m k) -> a k m", k=4))
+
+        xg = const.tile([P, D], BF16, name="xg", align_bytes=64)
+        xq = const.tile([P, GD, T], U32, name="xq", align_bytes=64)
+        xpl = const.tile([P, GD, T], U8, name="xpl", align_bytes=64)
+        xw = x_sb[:].bitcast(F32)
+        xgw = xg[:].bitcast(F32).rearrange("p (g t u) -> p g t u", g=GD, t=T, u=2)
+        for hb in range(2):
+            xt = psum.tile([P, 4, P], F32, name="xt", tag="y", bufs=3)
+            for gg in range(2):
+                g = 2 * hb + gg
+                for u in range(2):
+                    nc.tensor.transpose(xt[:, 2 * gg + u, :], xw[:, 256 * g + u : 256 * (g + 1) : 2], identf[:])
+            src = xt[:].rearrange("p (g u) t -> p g t u", u=2)
+            if hb == 0:
+                nc.vector.tensor_copy(out=xgw[:, 0:2], in_=src)
+            else:
+                nc.scalar.copy(out=xgw[:, 2:4], in_=src)
+        ct = psum.tile([P, 4, P], F32, name="ct", tag="y", bufs=3)
+        for k in range(4):
+            nc.tensor.transpose(ct[:, k, :], cwf[:, k, :], identf[:])
+        nc.vector.quantize_mx(
+            out=xq[:].rearrange("p g t -> p (g t)").bitcast(FP8X4),
+            scales=xpl[:].rearrange("p g t -> p (g t)"),
+            in_=xg[:],
+        )
+        coef = const.tile([P, 4, 64], F32, name="coef")
+        nc.vector.tensor_copy(out=coef[:], in_=ct[:, :, 0:64])
+        nc.vector.tensor_scalar_add(out=coef[:, 3, :], in0=coef[:, 3, :], scalar1=1.0)
+
+        hq = const.tile([P, GF, T], U32, name="hq", align_bytes=64)
+        hpl = const.tile([P, GF, T], U8, name="hpl", align_bytes=64)
+        ys = {}
+        accs = {}
+        sgs = {}
+        hTs = {}
+        sps = {}
+        hgs = {}
+
+        def pe_branch(b, br):
+            c, half = divmod(b, UNIT // KP)
+            wt = units[(c, br)]
+            pl = (gpl, upl)[br]
+            y = psum.tile([P, 4, T], F32, name="y", tag="y", bufs=3)
+            for a in range(4):
+                cu = KP * half + P * a
+                cf = KP * b + P * a
+                for g in range(GD):
+                    nc.tensor.matmul_mx(
+                        out=y[:, a, :],
+                        lhsT=wt[:, g, cu : cu + P].bitcast(FP8X4),
+                        lhsT_scale=pl[4 * g : P, cf : cf + P],
+                        rhs=xq[:, g, :].bitcast(FP8X4),
+                        rhs_scale=xpl[:, g, :],
+                        start=(g == 0),
+                        stop=(g == GD - 1),
+                    )
+            ys[(b, br)] = y
+
+        def act_first(b, br):
+            y = ys[(b, br)]
+            acc = work.tile([P, 4, T], F32, name="acc%d" % br)
+            ti = 32 * br + 4 * b
+            for a in range(4):
+                nc.scalar.activation(out=acc[:, a, :], in_=y[:, a, :], func=ACT.Copy, scale=coef[:, 3, ti + a : ti + a + 1])
+            accs[(b, br)] = acc
+
+        def vec_taps(b, br):
+            y = ys[(b, br)]
+            acc = accs[(b, br)]
+            ti = 32 * br + 4 * b
+            for s in (1, 2, 3):
+                for a in (3, 2, 1, 0):
+                    nc.vector.scalar_tensor_tensor(
+                        out=acc[:, a, s:T],
+                        in0=y[:, a, 0 : T - s],
+                        scalar=coef[:, 3 - s, ti + a : ti + a + 1],
+                        in1=acc[:, a, s:T],
+                        op0=ALU.mult,
+                        op1=ALU.add,
+                    )
+
+        def silu(b):
+            sg = work.tile([P, 4, T], F32, name="sg")
+            nc.scalar.activation(out=sg[:], in_=accs[(b, 0)][:], func=ACT.Silu)
+            sgs[b] = sg
+
+        def mul(b):
+            hT = work.tile([P, 4, T], BF16, name="hT")
+            nc.vector.tensor_tensor(out=hT[:], in0=accs[(b, 1)][:], in1=sgs[b][:], op=ALU.mult)
+            hTs[b] = hT
+
+        def select(b):
+            sp = psum.tile([P, 4, T], F32, name="sp", tag="sp", bufs=1)
+            for j in range(4):
+                for a in range(4):
+                    nc.tensor.matmul(out=sp[:, j, :], lhsT=sel[:, j, a, :], rhs=hTs[b][:, a, :], start=(a == 0), stop=(a == 3))
+            sps[b] = sp
+
+        def regroup(b):
+            hg = work.tile([P, T, 4], BF16, name="hg", align_bytes=64)
+            nc.scalar.copy(out=hg[:], in_=sps[b][:].rearrange("p j t -> p t j"))
+            hgs[b] = hg
+
+        def quant(b):
+            nc.vector.quantize_mx(
+                out=hq[:, b, :].bitcast(FP8X4),
+                scales=hpl[:, b, :],
+                in_=hgs[b][:].rearrange("p t j -> p (t j)"),
+            )
+
+        outs = []
+        for n in range(4):
+            o = psum.tile([P, KP], F32, name="o%d" % n, tag="o%d" % n, bufs=1)
+            outs.append(o)
+
+        def down(b):
+            for n in range(4):
+                nc.tensor.matmul_mx(
+                    out=outs[n][:],
+                    lhsT=hq[:, b, :].bitcast(FP8X4),
+                    lhsT_scale=hpl[:, b, :],
+                    rhs=dws[(b, n)].bitcast(FP8X4),
+                    rhs_scale=dpl[4 * (b % 4) : P, b // 4, KP * n : KP * (n + 1)],
+                    start=(b == 0),
+                    stop=(b == GF - 1),
+                )
+
+        pe_branch(0, 0)
+        act_first(0, 0)
+        pe_branch(0, 1)
+        act_first(0, 1)
+        for b in range(GF):
+            if b + 1 < GF:
+                pe_branch(b + 1, 0)
+                act_first(b + 1, 0)
+            vec_taps(b, 0)
+            if b == GF - 1:
+                down(0)
+            if b > 0:
+                select(b - 1)
+            silu(b)
+            if b > 0:
+                regroup(b - 1)
+            if b + 1 < GF:
+                pe_branch(b + 1, 1)
+                act_first(b + 1, 1)
+            vec_taps(b, 1)
+            mul(b)
+            if b > 0:
+                quant(b - 1)
+            if b == 0:
+                load_unit(RING)
+                load_unit(RING + 1)
+                load_down()
+        for b in (1, 2, 3, 4):
+            down(b)
+        select(GF - 1)
+        regroup(GF - 1)
+        quant(GF - 1)
+        for b in (5, 6, 7):
+            down(b)
+
+        osb = const.tile([P, D], F32, name="osb")
+        of = out.rearrange("b t d -> (b t) d")
+        for h in range(2):
+            nc.vector.tensor_copy(out=osb[:, KP * 2 * h : KP * (2 * h + 1)], in_=outs[2 * h][:])
+            nc.scalar.copy(out=osb[:, KP * (2 * h + 1) : KP * (2 * h + 2)], in_=outs[2 * h + 1][:])
+            nc.sync.dma_start(out=of[:, 2 * KP * h : 2 * KP * (h + 1)], in_=osb[:, 2 * KP * h : 2 * KP * (h + 1)])

@@ -49,12 +49,11 @@ def tile_canonglufeedforwardlayer_w_kernel(tc, x, wg_w, wg_s, wu_w, wu_s, wd_w, 
         nc.sync.dma_start(out=x_sb[:], in_=x.rearrange("b t d -> (b t) d"))
         nc.scalar.dma_start(out=cw_sb[0:64, :], in_=conv_w.rearrange("(a m) k -> a (m k)", m=P))
         nc.scalar.activation(out=warm[:, 4:8], in_=warm[:, 0:4], func=ACT.Silu)
-        for pl, sc in ((gpl, wg_s), (upl, wu_s)):
-            for q in range(4):
-                nc.sync.dma_start(
-                    out=pl[32 * q : 32 * q + 16, :].bitcast(I32),
-                    in_=sc[:, 4 * q : 4 * q + 4, :].bitcast(I32),
-                )
+        for q in range(4):
+            nc.sync.dma_start(
+                out=gpl[32 * q : 32 * q + 16, :].bitcast(I32),
+                in_=wg_s[:, 4 * q : 4 * q + 4, :].bitcast(I32),
+            )
 
         wviews = (
             wg_w.rearrange("g p n t -> p g (n t)").bitcast(I32),
@@ -70,13 +69,14 @@ def tile_canonglufeedforwardlayer_w_kernel(tc, x, wg_w, wg_s, wu_w, wu_s, wd_w, 
 
         dws = {}
 
+        def load_down_scales(h):
+            for q in range(4):
+                nc.sync.dma_start(
+                    out=dpl[32 * q : 32 * q + 16, h, :].bitcast(I32),
+                    in_=wd_s[4 * h : 4 * h + 4, 4 * q : 4 * q + 4, :].bitcast(I32),
+                )
+
         def load_down():
-            for h in range(2):
-                for q in range(4):
-                    nc.sync.dma_start(
-                        out=dpl[32 * q : 32 * q + 16, h, :].bitcast(I32),
-                        in_=wd_s[4 * h : 4 * h + 4, 4 * q : 4 * q + 4, :].bitcast(I32),
-                    )
             for b in range(GF):
                 src = wd_w[b].rearrange("p n t -> p (n t)").bitcast(I32)
                 parts = 2 if b == GF - 1 else 1
@@ -87,8 +87,19 @@ def tile_canonglufeedforwardlayer_w_kernel(tc, x, wg_w, wg_s, wu_w, wu_s, wd_w, 
                     for n in range(w * i // KP, w * (i + 1) // KP):
                         dws[(b, n)] = dw[:, KP * n - w * i : KP * (n + 1) - w * i]
 
-        for i in range(RING):
-            load_unit(i)
+        load_unit(0)
+        for q in (2, 3, 0, 1):
+            nc.scalar.dma_start(
+                out=upl[32 * q : 32 * q + 16, :].bitcast(F32),
+                in_=wu_s[:, 4 * q : 4 * q + 4, :].bitcast(F32),
+            )
+        load_unit(1)
+        load_unit(2)
+        load_unit(3)
+        load_down_scales(0)
+        load_unit(4)
+        load_down_scales(1)
+        load_unit(5)
 
         identf = const.tile([P, P], F32, name="identf")
         make_identity(nc, identf[:])

@@ -179,11 +179,11 @@ def tile_canonglufeedforwardlayer_w_kernel(tc, x, wg_w, wg_s, wu_w, wu_s, wd_w, 
                 nc.scalar.activation(out=acc[:, a, :], in_=y[:, a, :], func=ACT.Copy, scale=coef[:, 3, ti + a : ti + a + 1])
             accs[(b, br)] = acc
 
-        def vec_taps(b, br):
+        def vec_taps(b, br, shifts):
             y = ys[(b, br)]
             acc = accs[(b, br)]
             ti = 32 * br + 4 * b
-            for s in (1, 2, 3):
+            for s in shifts:
                 for a in (3, 2, 1, 0):
                     nc.vector.scalar_tensor_tensor(
                         out=acc[:, a, s:T],
@@ -201,7 +201,7 @@ def tile_canonglufeedforwardlayer_w_kernel(tc, x, wg_w, wg_s, wu_w, wu_s, wd_w, 
 
         def mul(b):
             hT = work.tile([P, 4, T], BF16, name="hT")
-            nc.vector.tensor_tensor(out=hT[:], in0=accs[(b, 1)][:], in1=sgs[b][:], op=ALU.mult)
+            nc.gpsimd.tensor_tensor(out=hT[:], in0=accs[(b, 1)][:], in1=sgs[b][:], op=ALU.mult)
             hTs[b] = hT
 
         def select(b):
@@ -248,7 +248,7 @@ def tile_canonglufeedforwardlayer_w_kernel(tc, x, wg_w, wg_s, wu_w, wu_s, wd_w, 
             if b + 1 < GF:
                 pe_branch(b + 1, 0)
                 act_first(b + 1, 0)
-            vec_taps(b, 0)
+            vec_taps(b, 0, (1, 2, 3))
             if b == GF - 1:
                 down(0)
             if b > 0:
@@ -259,10 +259,11 @@ def tile_canonglufeedforwardlayer_w_kernel(tc, x, wg_w, wg_s, wu_w, wu_s, wd_w, 
             if b + 1 < GF:
                 pe_branch(b + 1, 1)
                 act_first(b + 1, 1)
-            vec_taps(b, 1)
-            mul(b)
+            vec_taps(b, 1, (1, 2))
             if b > 0:
                 quant(b - 1)
+            vec_taps(b, 1, (3,))
+            mul(b)
             if b == 0:
                 load_unit(RING)
                 load_unit(RING + 1)

@@ -179,11 +179,11 @@ def tile_canonglufeedforwardlayer_w_kernel(tc, x, wg_w, wg_s, wu_w, wu_s, wd_w, 
                 nc.scalar.activation(out=acc[:, a, :], in_=y[:, a, :], func=ACT.Copy, scale=coef[:, 3, ti + a : ti + a + 1])
             accs[(b, br)] = acc
 
-        def vec_taps(b, br, shifts):
+        def vec_taps(b, br):
             y = ys[(b, br)]
             acc = accs[(b, br)]
             ti = 32 * br + 4 * b
-            for s in shifts:
+            for s in (1, 2, 3):
                 for a in (3, 2, 1, 0):
                     nc.vector.scalar_tensor_tensor(
                         out=acc[:, a, s:T],
@@ -201,7 +201,7 @@ def tile_canonglufeedforwardlayer_w_kernel(tc, x, wg_w, wg_s, wu_w, wu_s, wd_w, 
 
         def mul(b):
             hT = work.tile([P, 4, T], BF16, name="hT")
-            nc.gpsimd.tensor_tensor(out=hT[:], in0=accs[(b, 1)][:], in1=sgs[b][:], op=ALU.mult)
+            nc.vector.tensor_tensor(out=hT[:], in0=accs[(b, 1)][:], in1=sgs[b][:], op=ALU.mult)
             hTs[b] = hT
 
         def select(b):
@@ -240,40 +240,48 @@ def tile_canonglufeedforwardlayer_w_kernel(tc, x, wg_w, wg_s, wu_w, wu_s, wd_w, 
                     stop=(b == GF - 1),
                 )
 
-        pe_branch(0, 0)
-        act_first(0, 0)
-        pe_branch(0, 1)
-        act_first(0, 1)
-        for b in range(GF):
-            if b + 1 < GF:
-                pe_branch(b + 1, 0)
-                act_first(b + 1, 0)
-            vec_taps(b, 0, (1, 2, 3))
-            if b == GF - 1:
-                down(0)
-            if b > 0:
-                select(b - 1)
-            silu(b)
-            if b > 0:
-                regroup(b - 1)
-            if b + 1 < GF:
-                pe_branch(b + 1, 1)
-                act_first(b + 1, 1)
-            vec_taps(b, 1, (1, 2))
-            if b > 0:
-                quant(b - 1)
-            vec_taps(b, 1, (3,))
-            mul(b)
-            if b == 0:
+        for c in range(NUNIT):
+            b0 = 2 * c
+            b1 = b0 + 1
+            pe_branch(b0, 0)
+            act_first(b0, 0)
+            if c > 0:
+                select(b0 - 2)
+                regroup(b0 - 2)
+            pe_branch(b1, 0)
+            act_first(b1, 0)
+            vec_taps(b0, 0)
+            if c > 0:
+                quant(b0 - 2)
+            silu(b0)
+            if c > 0:
+                select(b0 - 1)
+                regroup(b0 - 1)
+            vec_taps(b1, 0)
+            if c > 0:
+                quant(b0 - 1)
+            pe_branch(b0, 1)
+            act_first(b0, 1)
+            silu(b1)
+            pe_branch(b1, 1)
+            act_first(b1, 1)
+            vec_taps(b0, 1)
+            mul(b0)
+            vec_taps(b1, 1)
+            mul(b1)
+            if c == 0:
                 load_unit(RING)
                 load_unit(RING + 1)
                 load_down()
-        for b in (1, 2, 3, 4):
-            down(b)
+        down(0)
+        select(GF - 2)
+        regroup(GF - 2)
+        quant(GF - 2)
+        down(1)
         select(GF - 1)
         regroup(GF - 1)
         quant(GF - 1)
-        for b in (5, 6, 7):
+        for b in range(2, GF):
             down(b)
 
         osb = const.tile([P, D], F32, name="osb")

@@ -39,21 +39,16 @@ def tile_canonglufeedforwardlayer_w_kernel(tc, x, wg_w, wg_s, wu_w, wu_s, wd_w, 
         dpl = const.tile([P, 2, D], U8, name="dpl", align_bytes=64)
         cw_sb = const.tile([P, 4 * P], BF16, name="cw_sb")
         warm = const.tile([P, 8], F32, name="warm")
-        nc.vector.memset(cw_sb[:].bitcast(I32), 0)
         nc.vector.memset(gpl[:].bitcast(I32), 0)
-        nc.vector.memset(upl[:].bitcast(I32), 0)
+        nc.vector.memset(cw_sb[:].bitcast(I32), 0)
         nc.vector.memset(warm[:], 0.0)
+        nc.vector.memset(upl[:].bitcast(I32), 0)
         nc.vector.memset(dpl[:].rearrange("p h n -> p (h n)").bitcast(I32), 0)
 
         x_sb = const.tile([P, D], BF16, name="x_sb")
         nc.sync.dma_start(out=x_sb[:], in_=x.rearrange("b t d -> (b t) d"))
         nc.scalar.dma_start(out=cw_sb[0:64, :], in_=conv_w.rearrange("(a m) k -> a (m k)", m=P))
         nc.scalar.activation(out=warm[:, 4:8], in_=warm[:, 0:4], func=ACT.Silu)
-        for q in range(4):
-            nc.sync.dma_start(
-                out=gpl[32 * q : 32 * q + 16, :].bitcast(I32),
-                in_=wg_s[:, 4 * q : 4 * q + 4, :].bitcast(I32),
-            )
 
         wviews = (
             wg_w.rearrange("g p n t -> p g (n t)").bitcast(I32),
@@ -70,10 +65,10 @@ def tile_canonglufeedforwardlayer_w_kernel(tc, x, wg_w, wg_s, wu_w, wu_s, wd_w, 
         dws = {}
 
         def load_down_scales(h):
-            for q in range(4):
-                nc.sync.dma_start(
-                    out=dpl[32 * q : 32 * q + 16, h, :].bitcast(I32),
-                    in_=wd_s[4 * h : 4 * h + 4, 4 * q : 4 * q + 4, :].bitcast(I32),
+            for q in (0, 2, 1, 3):
+                nc.gpsimd.dma_start(
+                    out=dpl[32 * q : 32 * q + 16, h, :].bitcast(F32),
+                    in_=wd_s[4 * h : 4 * h + 4, 4 * q : 4 * q + 4, :].bitcast(F32),
                 )
 
         def load_down():
@@ -87,22 +82,17 @@ def tile_canonglufeedforwardlayer_w_kernel(tc, x, wg_w, wg_s, wu_w, wu_s, wd_w, 
                     for n in range(w * i // KP, w * (i + 1) // KP):
                         dws[(b, n)] = dw[:, KP * n - w * i : KP * (n + 1) - w * i]
 
-        load_unit(0)
-        for q in (2, 3, 0, 1):
-            nc.scalar.dma_start(
-                out=upl[32 * q : 32 * q + 16, :].bitcast(F32),
-                in_=wu_s[:, 4 * q : 4 * q + 4, :].bitcast(F32),
-            )
-        load_unit(1)
-        load_unit(2)
-        load_unit(3)
-        load_down_scales(0)
-        load_unit(4)
-        load_down_scales(1)
-        load_unit(5)
+        for i in range(RING):
+            load_unit(i)
 
         identf = const.tile([P, P], F32, name="identf")
         make_identity(nc, identf[:])
+        for pl, sc in ((gpl, wg_s), (upl, wu_s)):
+            for q in (0, 2, 1, 3):
+                nc.gpsimd.dma_start(
+                    out=pl[32 * q : 32 * q + 16, :].bitcast(F32),
+                    in_=sc[:, 4 * q : 4 * q + 4, :].bitcast(F32),
+                )
         sel = const.tile([P, 4, 4, P], BF16, name="sel")
         nc.gpsimd.memset(sel[:].rearrange("m j a p -> m (j a p)").bitcast(F32), 0.0)
         for a in range(4):
@@ -110,6 +100,8 @@ def tile_canonglufeedforwardlayer_w_kernel(tc, x, wg_w, wg_s, wu_w, wu_s, wd_w, 
                 out=sel[:, :, a, 32 * a : 32 * a + 32],
                 in_=identf[:].rearrange("m (q j) -> m j q", j=4),
             )
+        load_down_scales(0)
+        load_down_scales(1)
 
         cwf = const.tile([P, 4, P], F32, name="cwf")
         nc.vector.tensor_copy(out=cwf[:], in_=cw_sb[:].rearrange("a (m k) -> a k m", k=4))

@@ -22,6 +22,7 @@ GF = F // KP
 UNIT = 1024
 NUNIT = F // UNIT
 RING = 6
+LAST_PIECES = (1024, 512, 512)
 FLOPS = 3 * 2 * T * D * F
 
 
@@ -74,13 +75,14 @@ def tile_canonglufeedforwardlayer_w_kernel(tc, x, wg_w, wg_s, wu_w, wu_s, wd_w, 
         def load_down():
             for b in range(GF):
                 src = wd_w[b].rearrange("p n t -> p (n t)").bitcast(I32)
-                parts = 2 if b == GF - 1 else 1
-                w = D // parts
-                for i in range(parts):
+                widths = LAST_PIECES if b == GF - 1 else (D,)
+                lo = 0
+                for i, w in enumerate(widths):
                     dw = const.tile([P, w], U32, name="dw%d_%d" % (b, i), align_bytes=64)
-                    nc.sync.dma_start(out=dw[:].bitcast(I32), in_=src[:, w * i : w * (i + 1)])
-                    for n in range(w * i // KP, w * (i + 1) // KP):
-                        dws[(b, n)] = dw[:, KP * n - w * i : KP * (n + 1) - w * i]
+                    nc.sync.dma_start(out=dw[:].bitcast(I32), in_=src[:, lo : lo + w])
+                    for n in range(lo // KP, (lo + w) // KP):
+                        dws[(b, n)] = dw[:, KP * n - lo : KP * (n + 1) - lo]
+                    lo += w
 
         for i in range(RING):
             load_unit(i)
@@ -278,7 +280,12 @@ def tile_canonglufeedforwardlayer_w_kernel(tc, x, wg_w, wg_s, wu_w, wu_s, wd_w, 
 
         osb = const.tile([P, D], F32, name="osb")
         of = out.rearrange("b t d -> (b t) d")
-        for h in range(2):
-            nc.vector.tensor_copy(out=osb[:, KP * 2 * h : KP * (2 * h + 1)], in_=outs[2 * h][:])
-            nc.scalar.copy(out=osb[:, KP * (2 * h + 1) : KP * (2 * h + 2)], in_=outs[2 * h + 1][:])
-            nc.sync.dma_start(out=of[:, 2 * KP * h : 2 * KP * (h + 1)], in_=osb[:, 2 * KP * h : 2 * KP * (h + 1)])
+        lo = 0
+        for w in LAST_PIECES:
+            for n in range(lo // KP, (lo + w) // KP):
+                if n % 2 == 0:
+                    nc.vector.tensor_copy(out=osb[:, KP * n : KP * (n + 1)], in_=outs[n][:])
+                else:
+                    nc.scalar.copy(out=osb[:, KP * n : KP * (n + 1)], in_=outs[n][:])
+            nc.sync.dma_start(out=of[:, lo : lo + w], in_=osb[:, lo : lo + w])
+            lo += w

@@ -22,7 +22,13 @@ GF = F // KP
 UNIT = 1024
 NUNIT = F // UNIT
 RING = 6
-LAST_PIECES = (1024, 512, 512)
+DOWN_PIECES = tuple((b, 0, D) for b in range(GF - 2)) + (
+    (GF - 2, 0, 1024),
+    (GF - 1, 0, 1024),
+    (GF - 2, 1024, 1024),
+    (GF - 1, 1024, 512),
+    (GF - 1, 1536, 512),
+)
 FLOPS = 3 * 2 * T * D * F
 
 
@@ -73,16 +79,12 @@ def tile_canonglufeedforwardlayer_w_kernel(tc, x, wg_w, wg_s, wu_w, wu_s, wd_w, 
                 )
 
         def load_down():
-            for b in range(GF):
+            for b, lo, w in DOWN_PIECES:
                 src = wd_w[b].rearrange("p n t -> p (n t)").bitcast(I32)
-                widths = LAST_PIECES if b == GF - 1 else (D,)
-                lo = 0
-                for i, w in enumerate(widths):
-                    dw = const.tile([P, w], U32, name="dw%d_%d" % (b, i), align_bytes=64)
-                    nc.sync.dma_start(out=dw[:].bitcast(I32), in_=src[:, lo : lo + w])
-                    for n in range(lo // KP, (lo + w) // KP):
-                        dws[(b, n)] = dw[:, KP * n - lo : KP * (n + 1) - lo]
-                    lo += w
+                dw = const.tile([P, w], U32, name="dw%d_%d" % (b, lo), align_bytes=64)
+                nc.sync.dma_start(out=dw[:].bitcast(I32), in_=src[:, lo : lo + w])
+                for n in range(lo // KP, (lo + w) // KP):
+                    dws[(b, n)] = dw[:, KP * n - lo : KP * (n + 1) - lo]
 
         for i in range(RING):
             load_unit(i)
@@ -222,8 +224,9 @@ def tile_canonglufeedforwardlayer_w_kernel(tc, x, wg_w, wg_s, wu_w, wu_s, wd_w, 
             o = psum.tile([P, KP], F32, name="o%d" % n, tag="o%d" % n, bufs=1)
             outs.append(o)
 
-        def down(b):
-            for n in range(4):
+        def down(piece):
+            b, lo, w = piece
+            for n in range(lo // KP, (lo + w) // KP):
                 nc.tensor.matmul_mx(
                     out=outs[n][:],
                     lhsT=hq[:, b, :].bitcast(FP8X4),
@@ -267,25 +270,24 @@ def tile_canonglufeedforwardlayer_w_kernel(tc, x, wg_w, wg_s, wu_w, wu_s, wd_w, 
                 load_unit(RING)
                 load_unit(RING + 1)
                 load_down()
-        down(0)
+        down(DOWN_PIECES[0])
         select(GF - 2)
         regroup(GF - 2)
         quant(GF - 2)
-        down(1)
+        down(DOWN_PIECES[1])
         select(GF - 1)
         regroup(GF - 1)
         quant(GF - 1)
-        for b in range(2, GF):
-            down(b)
+        for piece in DOWN_PIECES[2:]:
+            down(piece)
 
         osb = const.tile([P, D], F32, name="osb")
         of = out.rearrange("b t d -> (b t) d")
-        lo = 0
-        for w in LAST_PIECES:
-            for n in range(lo // KP, (lo + w) // KP):
-                if n % 2 == 0:
-                    nc.vector.tensor_copy(out=osb[:, KP * n : KP * (n + 1)], in_=outs[n][:])
-                else:
-                    nc.scalar.copy(out=osb[:, KP * n : KP * (n + 1)], in_=outs[n][:])
-            nc.sync.dma_start(out=of[:, lo : lo + w], in_=osb[:, lo : lo + w])
-            lo += w
+        for b, lo, w in DOWN_PIECES:
+            if b == GF - 1:
+                for n in range(lo // KP, (lo + w) // KP):
+                    if n % 2 == 0:
+                        nc.vector.tensor_copy(out=osb[:, KP * n : KP * (n + 1)], in_=outs[n][:])
+                    else:
+                        nc.scalar.copy(out=osb[:, KP * n : KP * (n + 1)], in_=outs[n][:])
+                nc.sync.dma_start(out=of[:, lo : lo + w], in_=osb[:, lo : lo + w])

@@ -16,278 +16,311 @@ P = 128
 T = 128
 D = 2048
 F = 4096
-KP = 512
-GD = D // KP
-GF = F // KP
-UNIT = 1024
-NUNIT = F // UNIT
-RING = 6
-DOWN_PIECES = tuple((b, 0, D) for b in range(GF - 2)) + (
-    (GF - 2, 0, 1024),
-    (GF - 1, 0, 1024),
-    (GF - 2, 1024, 1024),
-    (GF - 1, 1024, 512),
-    (GF - 1, 1536, 512),
+TAPS = 4
+PACK = 4
+GROUP = P * PACK
+D_GROUPS = D // GROUP
+F_GROUPS = F // GROUP
+OUT_BANKS = D // GROUP
+QUARTERS = GROUP // P
+QUADRANT = 32
+TILE_PLANES = 4
+PLANE_ROWS = 4
+LIVE_ROWS = TILE_PLANES * PLANE_ROWS
+CHANNEL_TILES = 2 * F // P
+UNIT = 2 * GROUP
+ROUNDS = F // UNIT
+UNIT_BUFFERS = 6
+RAW_BANKS = 3
+DOWN_PIECES = tuple((c, 0, D) for c in range(F_GROUPS - 2)) + (
+    (F_GROUPS - 2, 0, D // 2),
+    (F_GROUPS - 1, 0, D // 2),
+    (F_GROUPS - 2, D // 2, D // 2),
+    (F_GROUPS - 1, D // 2, GROUP),
+    (F_GROUPS - 1, D // 2 + GROUP, GROUP),
 )
+QUADRANT_ORDER = (0, 2, 1, 3)
 FLOPS = 3 * 2 * T * D * F
 
 
-def tile_canonglufeedforwardlayer_w_kernel(tc, x, wg_w, wg_s, wu_w, wu_s, wd_w, wd_s, conv_w, out):
+def tile_canonglufeedforwardlayer_w_kernel(
+    tc, x, w_gate_words, w_gate_scales, w_up_words, w_up_scales, w_down_words, w_down_scales, conv_w, out
+):
     nc = tc.nc
     with ExitStack() as ctx:
         ctx.enter_context(tc.manual_schedule())
-        const = ctx.enter_context(tc.tile_pool(name="const", bufs=1))
-        wpool = ctx.enter_context(tc.tile_pool(name="wpool", bufs=RING))
+        keep = ctx.enter_context(tc.tile_pool(name="keep", bufs=1))
+        unit_pool = ctx.enter_context(tc.tile_pool(name="unit_pool", bufs=UNIT_BUFFERS))
         work = ctx.enter_context(tc.tile_pool(name="work", bufs=2))
         psum = ctx.enter_context(tc.psum_pool(name="psum", bufs=1))
 
-        gpl = const.tile([P, F], U8, name="gpl", align_bytes=64)
-        upl = const.tile([P, F], U8, name="upl", align_bytes=64)
-        dpl = const.tile([P, 2, D], U8, name="dpl", align_bytes=64)
-        cw_sb = const.tile([P, 4 * P], BF16, name="cw_sb")
-        warm = const.tile([P, 8], F32, name="warm")
-        nc.vector.memset(gpl[:].bitcast(I32), 0)
-        nc.vector.memset(cw_sb[:].bitcast(I32), 0)
-        nc.vector.memset(warm[:], 0.0)
-        nc.vector.memset(upl[:].bitcast(I32), 0)
-        nc.vector.memset(dpl[:].rearrange("p h n -> p (h n)").bitcast(I32), 0)
+        gate_planes = keep.tile([P, F], U8, name="gate_planes", align_bytes=64)
+        up_planes = keep.tile([P, F], U8, name="up_planes", align_bytes=64)
+        down_planes = keep.tile([P, F_GROUPS // TILE_PLANES, D], U8, name="down_planes", align_bytes=64)
+        conv_rows = keep.tile([P, P * TAPS], BF16, name="conv_rows")
+        scratch = keep.tile([P, 8], F32, name="scratch")
+        nc.vector.memset(gate_planes[:].bitcast(I32), 0)
+        nc.vector.memset(conv_rows[:].bitcast(I32), 0)
+        nc.vector.memset(scratch[:], 0.0)
+        nc.vector.memset(up_planes[:].bitcast(I32), 0)
+        nc.vector.memset(down_planes[:].rearrange("p r n -> p (r n)").bitcast(I32), 0)
 
-        x_sb = const.tile([P, D], BF16, name="x_sb")
-        nc.sync.dma_start(out=x_sb[:], in_=x.rearrange("b t d -> (b t) d"))
-        nc.scalar.dma_start(out=cw_sb[0:64, :], in_=conv_w.rearrange("(a m) k -> a (m k)", m=P))
-        nc.scalar.activation(out=warm[:, 4:8], in_=warm[:, 0:4], func=ACT.Silu)
+        x_rows = keep.tile([P, D], BF16, name="x_rows")
+        nc.sync.dma_start(out=x_rows[:], in_=x.rearrange("b t d -> (b t) d"))
+        nc.scalar.dma_start(out=conv_rows[0:CHANNEL_TILES, :], in_=conv_w.rearrange("(i m) w -> i (m w)", m=P))
+        nc.scalar.activation(out=scratch[:, 4:8], in_=scratch[:, 0:4], func=ACT.Silu)
 
-        wviews = (
-            wg_w.rearrange("g p n t -> p g (n t)").bitcast(I32),
-            wu_w.rearrange("g p n t -> p g (n t)").bitcast(I32),
+        branch_words = (
+            w_gate_words.rearrange("g p n j -> p g (n j)").bitcast(I32),
+            w_up_words.rearrange("g p n j -> p g (n j)").bitcast(I32),
         )
         units = {}
 
-        def load_unit(i):
-            c, br = divmod(i, 2)
-            wt = wpool.tile([P, GD, UNIT], U32, name="wt", align_bytes=64)
-            nc.sync.dma_start(out=wt[:].bitcast(I32), in_=wviews[br][:, :, UNIT * c : UNIT * (c + 1)])
-            units[(c, br)] = wt
-
-        dws = {}
-
-        def load_down_scales(h):
-            for q in (0, 2, 1, 3):
-                nc.gpsimd.dma_start(
-                    out=dpl[32 * q : 32 * q + 16, h, :].bitcast(F32),
-                    in_=wd_s[4 * h : 4 * h + 4, 4 * q : 4 * q + 4, :].bitcast(F32),
-                )
-
-        def load_down():
-            for b, lo, w in DOWN_PIECES:
-                src = wd_w[b].rearrange("p n t -> p (n t)").bitcast(I32)
-                dw = const.tile([P, w], U32, name="dw%d_%d" % (b, lo), align_bytes=64)
-                nc.sync.dma_start(out=dw[:].bitcast(I32), in_=src[:, lo : lo + w])
-                for n in range(lo // KP, (lo + w) // KP):
-                    dws[(b, n)] = dw[:, KP * n - lo : KP * (n + 1) - lo]
-
-        for i in range(RING):
-            load_unit(i)
-
-        identf = const.tile([P, P], F32, name="identf")
-        make_identity(nc, identf[:])
-        for pl, sc in ((gpl, wg_s), (upl, wu_s)):
-            for q in (0, 2, 1, 3):
-                nc.gpsimd.dma_start(
-                    out=pl[32 * q : 32 * q + 16, :].bitcast(F32),
-                    in_=sc[:, 4 * q : 4 * q + 4, :].bitcast(F32),
-                )
-        sel = const.tile([P, 4, 4, P], BF16, name="sel")
-        nc.gpsimd.memset(sel[:].rearrange("m j a p -> m (j a p)").bitcast(F32), 0.0)
-        for a in range(4):
-            nc.gpsimd.tensor_copy(
-                out=sel[:, :, a, 32 * a : 32 * a + 32],
-                in_=identf[:].rearrange("m (q j) -> m j q", j=4),
+        def load_unit(index):
+            rnd, branch = divmod(index, 2)
+            unit_words = unit_pool.tile([P, D_GROUPS, UNIT], U32, name="unit_words", align_bytes=64)
+            nc.sync.dma_start(
+                out=unit_words[:].bitcast(I32), in_=branch_words[branch][:, :, UNIT * rnd : UNIT * (rnd + 1)]
             )
-        load_down_scales(0)
-        load_down_scales(1)
+            units[(rnd, branch)] = unit_words
 
-        cwf = const.tile([P, 4, P], F32, name="cwf")
-        nc.vector.tensor_copy(out=cwf[:], in_=cw_sb[:].rearrange("a (m k) -> a k m", k=4))
+        down_words = {}
 
-        xg = const.tile([P, D], BF16, name="xg", align_bytes=64)
-        xq = const.tile([P, GD, T], U32, name="xq", align_bytes=64)
-        xpl = const.tile([P, GD, T], U8, name="xpl", align_bytes=64)
-        xw = x_sb[:].bitcast(F32)
-        xgw = xg[:].bitcast(F32).rearrange("p (g t u) -> p g t u", g=GD, t=T, u=2)
-        for hb in range(2):
-            xt = psum.tile([P, 4, P], F32, name="xt", tag="y", bufs=3)
-            for gg in range(2):
-                g = 2 * hb + gg
+        def load_down_planes(col_range):
+            for quad in QUADRANT_ORDER:
+                nc.gpsimd.dma_start(
+                    out=down_planes[QUADRANT * quad : QUADRANT * quad + LIVE_ROWS, col_range, :].bitcast(F32),
+                    in_=w_down_scales[
+                        TILE_PLANES * col_range : TILE_PLANES * (col_range + 1),
+                        PLANE_ROWS * quad : PLANE_ROWS * (quad + 1),
+                        :,
+                    ].bitcast(F32),
+                )
+
+        def load_down_words():
+            for c, first, cols in DOWN_PIECES:
+                source = w_down_words[c].rearrange("p n j -> p (n j)").bitcast(I32)
+                words = keep.tile([P, cols], U32, name="down_words_%d_%d" % (c, first), align_bytes=64)
+                nc.sync.dma_start(out=words[:].bitcast(I32), in_=source[:, first : first + cols])
+                for n in range(first // GROUP, (first + cols) // GROUP):
+                    down_words[(c, n)] = words[:, GROUP * n - first : GROUP * (n + 1) - first]
+
+        for index in range(UNIT_BUFFERS):
+            load_unit(index)
+
+        identity = keep.tile([P, P], F32, name="identity")
+        make_identity(nc, identity[:])
+        for planes, scales in ((gate_planes, w_gate_scales), (up_planes, w_up_scales)):
+            for quad in QUADRANT_ORDER:
+                nc.gpsimd.dma_start(
+                    out=planes[QUADRANT * quad : QUADRANT * quad + LIVE_ROWS, :].bitcast(F32),
+                    in_=scales[:, PLANE_ROWS * quad : PLANE_ROWS * (quad + 1), :].bitcast(F32),
+                )
+        selectors = keep.tile([P, PACK, QUARTERS, P], BF16, name="selectors")
+        nc.gpsimd.memset(selectors[:].rearrange("m j a p -> m (j a p)").bitcast(F32), 0.0)
+        for a in range(QUARTERS):
+            nc.gpsimd.tensor_copy(
+                out=selectors[:, :, a, (P // PACK) * a : (P // PACK) * (a + 1)],
+                in_=identity[:].rearrange("m (r j) -> m j r", j=PACK),
+            )
+        for col_range in range(F_GROUPS // TILE_PLANES):
+            load_down_planes(col_range)
+
+        conv_f32 = keep.tile([P, TAPS, P], F32, name="conv_f32")
+        nc.vector.tensor_copy(out=conv_f32[:], in_=conv_rows[:].rearrange("i (m w) -> i w m", w=TAPS))
+
+        x_grouped = keep.tile([P, D], BF16, name="x_grouped", align_bytes=64)
+        x_words = keep.tile([P, D_GROUPS, T], U32, name="x_words", align_bytes=64)
+        x_planes = keep.tile([P, D_GROUPS, T], U8, name="x_planes", align_bytes=64)
+        x_as_f32 = x_rows[:].bitcast(F32)
+        x_grouped_as_f32 = x_grouped[:].bitcast(F32).rearrange("p (g t u) -> p g t u", g=D_GROUPS, t=T, u=2)
+        for half in range(2):
+            x_t = psum.tile([P, 4, P], F32, name="x_t", tag="raw", bufs=RAW_BANKS)
+            for g in (2 * half, 2 * half + 1):
                 for u in range(2):
-                    nc.tensor.transpose(xt[:, 2 * gg + u, :], xw[:, 256 * g + u : 256 * (g + 1) : 2], identf[:])
-            src = xt[:].rearrange("p (g u) t -> p g t u", u=2)
-            if hb == 0:
-                nc.vector.tensor_copy(out=xgw[:, 0:2], in_=src)
-            else:
-                nc.scalar.copy(out=xgw[:, 2:4], in_=src)
-        ct = psum.tile([P, 4, P], F32, name="ct", tag="y", bufs=3)
-        for k in range(4):
-            nc.tensor.transpose(ct[:, k, :], cwf[:, k, :], identf[:])
-        nc.vector.quantize_mx(
-            out=xq[:].rearrange("p g t -> p (g t)").bitcast(FP8X4),
-            scales=xpl[:].rearrange("p g t -> p (g t)"),
-            in_=xg[:],
-        )
-        coef = const.tile([P, 4, 64], F32, name="coef")
-        nc.vector.tensor_copy(out=coef[:], in_=ct[:, :, 0:64])
-        nc.vector.tensor_scalar_add(out=coef[:, 3, :], in0=coef[:, 3, :], scalar1=1.0)
-
-        hq = const.tile([P, GF, T], U32, name="hq", align_bytes=64)
-        hpl = const.tile([P, GF, T], U8, name="hpl", align_bytes=64)
-        ys = {}
-        accs = {}
-        sgs = {}
-        hTs = {}
-        sps = {}
-        hgs = {}
-
-        def pe_branch(b, br):
-            c, half = divmod(b, UNIT // KP)
-            wt = units[(c, br)]
-            pl = (gpl, upl)[br]
-            y = psum.tile([P, 4, T], F32, name="y", tag="y", bufs=3)
-            for a in range(4):
-                cu = KP * half + P * a
-                cf = KP * b + P * a
-                for g in range(GD):
-                    nc.tensor.matmul_mx(
-                        out=y[:, a, :],
-                        lhsT=wt[:, g, cu : cu + P].bitcast(FP8X4),
-                        lhsT_scale=pl[4 * g : P, cf : cf + P],
-                        rhs=xq[:, g, :].bitcast(FP8X4),
-                        rhs_scale=xpl[:, g, :],
-                        start=(g == 0),
-                        stop=(g == GD - 1),
+                    nc.tensor.transpose(
+                        x_t[:, 2 * (g % 2) + u, :],
+                        x_as_f32[:, (GROUP // 2) * g + u : (GROUP // 2) * (g + 1) : 2],
+                        identity[:],
                     )
-            ys[(b, br)] = y
+            side_by_side = x_t[:].rearrange("p (g u) t -> p g t u", u=2)
+            if half == 0:
+                nc.vector.tensor_copy(out=x_grouped_as_f32[:, 0:2], in_=side_by_side)
+            else:
+                nc.scalar.copy(out=x_grouped_as_f32[:, 2:4], in_=side_by_side)
+        conv_t = psum.tile([P, TAPS, P], F32, name="conv_t", tag="raw", bufs=RAW_BANKS)
+        for tap in range(TAPS):
+            nc.tensor.transpose(conv_t[:, tap, :], conv_f32[:, tap, :], identity[:])
+        nc.vector.quantize_mx(
+            out=x_words[:].rearrange("p g t -> p (g t)").bitcast(FP8X4),
+            scales=x_planes[:].rearrange("p g t -> p (g t)"),
+            in_=x_grouped[:],
+        )
+        taps = keep.tile([P, TAPS, CHANNEL_TILES], F32, name="taps")
+        nc.vector.tensor_copy(out=taps[:], in_=conv_t[:, :, 0:CHANNEL_TILES])
+        nc.vector.tensor_scalar_add(out=taps[:, TAPS - 1, :], in0=taps[:, TAPS - 1, :], scalar1=1.0)
 
-        def act_first(b, br):
-            y = ys[(b, br)]
-            acc = work.tile([P, 4, T], F32, name="acc%d" % br)
-            ti = 32 * br + 4 * b
-            for a in range(4):
-                nc.scalar.activation(out=acc[:, a, :], in_=y[:, a, :], func=ACT.Copy, scale=coef[:, 3, ti + a : ti + a + 1])
-            accs[(b, br)] = acc
+        h_words = keep.tile([P, F_GROUPS, T], U32, name="h_words", align_bytes=64)
+        h_planes = keep.tile([P, F_GROUPS, T], U8, name="h_planes", align_bytes=64)
+        raws = {}
+        convolved = {}
+        gate_acts = {}
+        h_by_channel = {}
+        h_moved = {}
+        h_grouped = {}
 
-        def vec_taps(b, br):
-            y = ys[(b, br)]
-            acc = accs[(b, br)]
-            ti = 32 * br + 4 * b
-            for s in (1, 2, 3):
-                for a in (3, 2, 1, 0):
+        def first_passes(c, branch):
+            rnd, part = divmod(c, UNIT // GROUP)
+            unit_words = units[(rnd, branch)]
+            planes = (gate_planes, up_planes)[branch]
+            raw = psum.tile([P, QUARTERS, T], F32, name="raw", tag="raw", bufs=RAW_BANKS)
+            for a in range(QUARTERS):
+                in_unit = GROUP * part + P * a
+                in_branch = GROUP * c + P * a
+                for g in range(D_GROUPS):
+                    nc.tensor.matmul_mx(
+                        out=raw[:, a, :],
+                        lhsT=unit_words[:, g, in_unit : in_unit + P].bitcast(FP8X4),
+                        lhsT_scale=planes[PLANE_ROWS * g : P, in_branch : in_branch + P],
+                        rhs=x_words[:, g, :].bitcast(FP8X4),
+                        rhs_scale=x_planes[:, g, :],
+                        start=(g == 0),
+                        stop=(g == D_GROUPS - 1),
+                    )
+            raws[(c, branch)] = raw
+
+        def present_term(c, branch):
+            raw = raws[(c, branch)]
+            conv = work.tile([P, QUARTERS, T], F32, name="conv%d" % branch)
+            tile0 = (F // P) * branch + QUARTERS * c
+            for a in range(QUARTERS):
+                nc.scalar.activation(
+                    out=conv[:, a, :],
+                    in_=raw[:, a, :],
+                    func=ACT.Copy,
+                    scale=taps[:, TAPS - 1, tile0 + a : tile0 + a + 1],
+                )
+            convolved[(c, branch)] = conv
+
+        def older_terms(c, branch):
+            raw = raws[(c, branch)]
+            conv = convolved[(c, branch)]
+            tile0 = (F // P) * branch + QUARTERS * c
+            for s in range(1, TAPS):
+                for a in reversed(range(QUARTERS)):
                     nc.vector.scalar_tensor_tensor(
-                        out=acc[:, a, s:T],
-                        in0=y[:, a, 0 : T - s],
-                        scalar=coef[:, 3 - s, ti + a : ti + a + 1],
-                        in1=acc[:, a, s:T],
+                        out=conv[:, a, s:T],
+                        in0=raw[:, a, 0 : T - s],
+                        scalar=taps[:, TAPS - 1 - s, tile0 + a : tile0 + a + 1],
+                        in1=conv[:, a, s:T],
                         op0=ALU.mult,
                         op1=ALU.add,
                     )
 
-        def silu(b):
-            sg = work.tile([P, 4, T], F32, name="sg")
-            nc.scalar.activation(out=sg[:], in_=accs[(b, 0)][:], func=ACT.Silu)
-            sgs[b] = sg
+        def gate_silu(c):
+            gate_act = work.tile([P, QUARTERS, T], F32, name="gate_act")
+            nc.scalar.activation(out=gate_act[:], in_=convolved[(c, 0)][:], func=ACT.Silu)
+            gate_acts[c] = gate_act
 
-        def mul(b):
-            hT = work.tile([P, 4, T], BF16, name="hT")
-            nc.vector.tensor_tensor(out=hT[:], in0=accs[(b, 1)][:], in1=sgs[b][:], op=ALU.mult)
-            hTs[b] = hT
+        def up_times_gate(c):
+            h_channel = work.tile([P, QUARTERS, T], BF16, name="h_channel")
+            nc.vector.tensor_tensor(out=h_channel[:], in0=convolved[(c, 1)][:], in1=gate_acts[c][:], op=ALU.mult)
+            h_by_channel[c] = h_channel
 
-        def select(b):
-            sp = psum.tile([P, 4, T], F32, name="sp", tag="sp", bufs=1)
-            for j in range(4):
-                for a in range(4):
-                    nc.tensor.matmul(out=sp[:, j, :], lhsT=sel[:, j, a, :], rhs=hTs[b][:, a, :], start=(a == 0), stop=(a == 3))
-            sps[b] = sp
+        def move_rows(c):
+            h_rows = psum.tile([P, PACK, T], F32, name="h_rows", tag="h_rows", bufs=1)
+            for j in range(PACK):
+                for a in range(QUARTERS):
+                    nc.tensor.matmul(
+                        out=h_rows[:, j, :],
+                        lhsT=selectors[:, j, a, :],
+                        rhs=h_by_channel[c][:, a, :],
+                        start=(a == 0),
+                        stop=(a == QUARTERS - 1),
+                    )
+            h_moved[c] = h_rows
 
-        def regroup(b):
-            hg = work.tile([P, T, 4], BF16, name="hg", align_bytes=64)
-            nc.scalar.copy(out=hg[:], in_=sps[b][:].rearrange("p j t -> p t j"))
-            hgs[b] = hg
+        def lay_words(c):
+            h_side_by_side = work.tile([P, T, PACK], BF16, name="h_side_by_side", align_bytes=64)
+            nc.scalar.copy(out=h_side_by_side[:], in_=h_moved[c][:].rearrange("p j t -> p t j"))
+            h_grouped[c] = h_side_by_side
 
-        def quant(b):
+        def quantise_h(c):
             nc.vector.quantize_mx(
-                out=hq[:, b, :].bitcast(FP8X4),
-                scales=hpl[:, b, :],
-                in_=hgs[b][:].rearrange("p t j -> p (t j)"),
+                out=h_words[:, c, :].bitcast(FP8X4),
+                scales=h_planes[:, c, :],
+                in_=h_grouped[c][:].rearrange("p t j -> p (t j)"),
             )
 
-        outs = []
-        for n in range(4):
-            o = psum.tile([P, KP], F32, name="o%d" % n, tag="o%d" % n, bufs=1)
-            outs.append(o)
+        out_banks = []
+        for n in range(OUT_BANKS):
+            out_bank = psum.tile([P, GROUP], F32, name="out_bank%d" % n, tag="out_bank%d" % n, bufs=1)
+            out_banks.append(out_bank)
 
-        def down(piece):
-            b, lo, w = piece
-            for n in range(lo // KP, (lo + w) // KP):
+        def down_passes(piece):
+            c, first, cols = piece
+            for n in range(first // GROUP, (first + cols) // GROUP):
                 nc.tensor.matmul_mx(
-                    out=outs[n][:],
-                    lhsT=hq[:, b, :].bitcast(FP8X4),
-                    lhsT_scale=hpl[:, b, :],
-                    rhs=dws[(b, n)].bitcast(FP8X4),
-                    rhs_scale=dpl[4 * (b % 4) : P, b // 4, KP * n : KP * (n + 1)],
-                    start=(b == 0),
-                    stop=(b == GF - 1),
+                    out=out_banks[n][:],
+                    lhsT=h_words[:, c, :].bitcast(FP8X4),
+                    lhsT_scale=h_planes[:, c, :],
+                    rhs=down_words[(c, n)].bitcast(FP8X4),
+                    rhs_scale=down_planes[PLANE_ROWS * (c % TILE_PLANES) : P, c // TILE_PLANES, GROUP * n : GROUP * (n + 1)],
+                    start=(c == 0),
+                    stop=(c == F_GROUPS - 1),
                 )
 
-        for c in range(NUNIT):
-            b0 = 2 * c
-            b1 = b0 + 1
-            pe_branch(b0, 0)
-            act_first(b0, 0)
-            if c > 0:
-                select(b0 - 2)
-                regroup(b0 - 2)
-            pe_branch(b1, 0)
-            act_first(b1, 0)
-            vec_taps(b0, 0)
-            if c > 0:
-                quant(b0 - 2)
-            silu(b0)
-            if c > 0:
-                select(b0 - 1)
-                regroup(b0 - 1)
-            vec_taps(b1, 0)
-            if c > 0:
-                quant(b0 - 1)
-            pe_branch(b0, 1)
-            act_first(b0, 1)
-            silu(b1)
-            pe_branch(b1, 1)
-            act_first(b1, 1)
-            vec_taps(b0, 1)
-            mul(b0)
-            vec_taps(b1, 1)
-            mul(b1)
-            if c == 0:
-                load_unit(RING)
-                load_unit(RING + 1)
-                load_down()
-        down(DOWN_PIECES[0])
-        select(GF - 2)
-        regroup(GF - 2)
-        quant(GF - 2)
-        down(DOWN_PIECES[1])
-        select(GF - 1)
-        regroup(GF - 1)
-        quant(GF - 1)
+        for rnd in range(ROUNDS):
+            c0 = 2 * rnd
+            c1 = c0 + 1
+            first_passes(c0, 0)
+            present_term(c0, 0)
+            if rnd > 0:
+                move_rows(c0 - 2)
+                lay_words(c0 - 2)
+            first_passes(c1, 0)
+            present_term(c1, 0)
+            older_terms(c0, 0)
+            if rnd > 0:
+                quantise_h(c0 - 2)
+            gate_silu(c0)
+            if rnd > 0:
+                move_rows(c0 - 1)
+                lay_words(c0 - 1)
+            older_terms(c1, 0)
+            if rnd > 0:
+                quantise_h(c0 - 1)
+            first_passes(c0, 1)
+            present_term(c0, 1)
+            gate_silu(c1)
+            first_passes(c1, 1)
+            present_term(c1, 1)
+            older_terms(c0, 1)
+            up_times_gate(c0)
+            older_terms(c1, 1)
+            up_times_gate(c1)
+            if rnd == 0:
+                load_unit(UNIT_BUFFERS)
+                load_unit(UNIT_BUFFERS + 1)
+                load_down_words()
+        down_passes(DOWN_PIECES[0])
+        move_rows(F_GROUPS - 2)
+        lay_words(F_GROUPS - 2)
+        quantise_h(F_GROUPS - 2)
+        down_passes(DOWN_PIECES[1])
+        move_rows(F_GROUPS - 1)
+        lay_words(F_GROUPS - 1)
+        quantise_h(F_GROUPS - 1)
         for piece in DOWN_PIECES[2:]:
-            down(piece)
+            down_passes(piece)
 
-        osb = const.tile([P, D], F32, name="osb")
-        of = out.rearrange("b t d -> (b t) d")
-        for b, lo, w in DOWN_PIECES:
-            if b == GF - 1:
-                for n in range(lo // KP, (lo + w) // KP):
+        out_rows = keep.tile([P, D], F32, name="out_rows")
+        out_flat = out.rearrange("b t d -> (b t) d")
+        for c, first, cols in DOWN_PIECES:
+            if c == F_GROUPS - 1:
+                for n in range(first // GROUP, (first + cols) // GROUP):
                     if n % 2 == 0:
-                        nc.vector.tensor_copy(out=osb[:, KP * n : KP * (n + 1)], in_=outs[n][:])
+                        nc.vector.tensor_copy(out=out_rows[:, GROUP * n : GROUP * (n + 1)], in_=out_banks[n][:])
                     else:
-                        nc.scalar.copy(out=osb[:, KP * n : KP * (n + 1)], in_=outs[n][:])
-                nc.sync.dma_start(out=of[:, lo : lo + w], in_=osb[:, lo : lo + w])
+                        nc.scalar.copy(out=out_rows[:, GROUP * n : GROUP * (n + 1)], in_=out_banks[n][:])
+                nc.sync.dma_start(out=out_flat[:, first : first + cols], in_=out_rows[:, first : first + cols])

@@ -303,15 +303,16 @@ def tile_canonglufeedforwardlayer_w_kernel(
                 load_unit(UNIT_BUFFERS)
                 load_unit(UNIT_BUFFERS + 1)
                 load_down_words()
-        down_passes(DOWN_PIECES[0])
+        for piece in DOWN_PIECES[0:4]:
+            down_passes(piece)
         move_rows(F_GROUPS - 2)
         lay_words(F_GROUPS - 2)
         quantise_h(F_GROUPS - 2)
-        down_passes(DOWN_PIECES[1])
+        down_passes(DOWN_PIECES[4])
         move_rows(F_GROUPS - 1)
         lay_words(F_GROUPS - 1)
         quantise_h(F_GROUPS - 1)
-        for piece in DOWN_PIECES[2:]:
+        for piece in DOWN_PIECES[5:]:
             down_passes(piece)
 
         out_rows = keep.tile([P, D], F32, name="out_rows")

@@ -39,7 +39,7 @@ DOWN_PIECES = tuple((c, 0, D) for c in range(F_GROUPS - 2)) + (
     (F_GROUPS - 1, D // 2, GROUP),
     (F_GROUPS - 1, D // 2 + GROUP, GROUP),
 )
-QUADRANT_ORDER = (0, 2, 1, 3)
+QUADRANT_ORDER = (0, 1, 2, 3)
 FLOPS = 3 * 2 * T * D * F
 
 

@@ -40,6 +40,7 @@ DOWN_PIECES = tuple((c, 0, D) for c in range(F_GROUPS - 2)) + (
     (F_GROUPS - 1, D // 2 + GROUP, GROUP),
 )
 QUADRANT_ORDER = (0, 1, 2, 3)
+DMA_ALIGN = 256
 FLOPS = 3 * 2 * T * D * F
 
 
@@ -54,9 +55,9 @@ def tile_canonglufeedforwardlayer_w_kernel(
         work = ctx.enter_context(tc.tile_pool(name="work", bufs=2))
         psum = ctx.enter_context(tc.psum_pool(name="psum", bufs=1))
 
-        gate_planes = keep.tile([P, F], U8, name="gate_planes", align_bytes=64)
-        up_planes = keep.tile([P, F], U8, name="up_planes", align_bytes=64)
-        down_planes = keep.tile([P, F_GROUPS // TILE_PLANES, D], U8, name="down_planes", align_bytes=64)
+        gate_planes = keep.tile([P, F], U8, name="gate_planes", align_bytes=DMA_ALIGN)
+        up_planes = keep.tile([P, F], U8, name="up_planes", align_bytes=DMA_ALIGN)
+        down_planes = keep.tile([P, F_GROUPS // TILE_PLANES, D], U8, name="down_planes", align_bytes=DMA_ALIGN)
         conv_rows = keep.tile([P, P * TAPS], BF16, name="conv_rows")
         scratch = keep.tile([P, 8], F32, name="scratch")
         nc.vector.memset(gate_planes[:].bitcast(I32), 0)
@@ -65,7 +66,7 @@ def tile_canonglufeedforwardlayer_w_kernel(
         nc.vector.memset(up_planes[:].bitcast(I32), 0)
         nc.vector.memset(down_planes[:].rearrange("p r n -> p (r n)").bitcast(I32), 0)
 
-        x_rows = keep.tile([P, D], BF16, name="x_rows")
+        x_rows = keep.tile([P, D], BF16, name="x_rows", align_bytes=DMA_ALIGN)
         nc.sync.dma_start(out=x_rows[:], in_=x.rearrange("b t d -> (b t) d"))
         nc.scalar.dma_start(out=conv_rows[0:CHANNEL_TILES, :], in_=conv_w.rearrange("(i m) w -> i (m w)", m=P))
         nc.scalar.activation(out=scratch[:, 4:8], in_=scratch[:, 0:4], func=ACT.Silu)
@@ -78,7 +79,7 @@ def tile_canonglufeedforwardlayer_w_kernel(
 
         def load_unit(index):
             rnd, branch = divmod(index, 2)
-            unit_words = unit_pool.tile([P, D_GROUPS, UNIT], U32, name="unit_words", align_bytes=64)
+            unit_words = unit_pool.tile([P, D_GROUPS, UNIT], U32, name="unit_words", align_bytes=DMA_ALIGN)
             nc.sync.dma_start(
                 out=unit_words[:].bitcast(I32), in_=branch_words[branch][:, :, UNIT * rnd : UNIT * (rnd + 1)]
             )
@@ -100,7 +101,7 @@ def tile_canonglufeedforwardlayer_w_kernel(
         def load_down_words():
             for c, first, cols in DOWN_PIECES:
                 source = w_down_words[c].rearrange("p n j -> p (n j)").bitcast(I32)
-                words = keep.tile([P, cols], U32, name="down_words_%d_%d" % (c, first), align_bytes=64)
+                words = keep.tile([P, cols], U32, name="down_words_%d_%d" % (c, first), align_bytes=DMA_ALIGN)
                 nc.sync.dma_start(out=words[:].bitcast(I32), in_=source[:, first : first + cols])
                 for n in range(first // GROUP, (first + cols) // GROUP):
                     down_words[(c, n)] = words[:, GROUP * n - first : GROUP * (n + 1) - first]
@@ -315,7 +316,7 @@ def tile_canonglufeedforwardlayer_w_kernel(
         for piece in DOWN_PIECES[5:]:
             down_passes(piece)
 
-        out_rows = keep.tile([P, D], F32, name="out_rows")
+        out_rows = keep.tile([P, D], F32, name="out_rows", align_bytes=DMA_ALIGN)
         out_flat = out.rearrange("b t d -> (b t) d")
         for c, first, cols in DOWN_PIECES:
             if c == F_GROUPS - 1:

@@ -39,7 +39,8 @@ DOWN_PIECES = tuple((c, 0, D) for c in range(F_GROUPS - 2)) + (
     (F_GROUPS - 1, D // 2, GROUP),
     (F_GROUPS - 1, D // 2 + GROUP, GROUP),
 )
-QUADRANT_ORDER = (0, 1, 2, 3)
+QUADRANT_ORDER = (0, 2, 1, 3)
+SKIPS = 12
 DMA_ALIGN = 256
 FLOPS = 3 * 2 * T * D * F
 
@@ -86,6 +87,16 @@ def tile_canonglufeedforwardlayer_w_kernel(
             units[(rnd, branch)] = unit_words
 
         down_words = {}
+        skipped = []
+        skip_bytes = keep.tile([P, SKIPS, 16], F32, name="skip_bytes")
+
+        def skip_four_engines(half):
+            first = (P // 2) * half + LIVE_ROWS
+            nc.gpsimd.dma_start(
+                out=skip_bytes[first : first + LIVE_ROWS, len(skipped), :],
+                in_=w_gate_scales[:, 0:PLANE_ROWS, 0:64].bitcast(F32),
+            )
+            skipped.append(half)
 
         def load_down_planes(col_range):
             for quad in QUADRANT_ORDER:
@@ -97,6 +108,7 @@ def tile_canonglufeedforwardlayer_w_kernel(
                         :,
                     ].bitcast(F32),
                 )
+                skip_four_engines(quad // 2)
 
         def load_down_words():
             for c, first, cols in DOWN_PIECES:
@@ -111,12 +123,17 @@ def tile_canonglufeedforwardlayer_w_kernel(
 
         identity = keep.tile([P, P], F32, name="identity")
         make_identity(nc, identity[:])
-        for planes, scales in ((gate_planes, w_gate_scales), (up_planes, w_up_scales)):
-            for quad in QUADRANT_ORDER:
-                nc.gpsimd.dma_start(
-                    out=planes[QUADRANT * quad : QUADRANT * quad + LIVE_ROWS, :].bitcast(F32),
-                    in_=scales[:, PLANE_ROWS * quad : PLANE_ROWS * (quad + 1), :].bitcast(F32),
-                )
+        for quad in range(P // QUADRANT):
+            nc.gpsimd.dma_start(
+                out=gate_planes[QUADRANT * quad : QUADRANT * quad + LIVE_ROWS, :].bitcast(F32),
+                in_=w_gate_scales[:, PLANE_ROWS * quad : PLANE_ROWS * (quad + 1), :].bitcast(F32),
+            )
+        for quad in QUADRANT_ORDER:
+            nc.gpsimd.dma_start(
+                out=up_planes[QUADRANT * quad : QUADRANT * quad + LIVE_ROWS, :].bitcast(F32),
+                in_=w_up_scales[:, PLANE_ROWS * quad : PLANE_ROWS * (quad + 1), :].bitcast(F32),
+            )
+            skip_four_engines(quad // 2)
         selectors = keep.tile([P, PACK, QUARTERS, P], BF16, name="selectors")
         nc.gpsimd.memset(selectors[:].rearrange("m j a p -> m (j a p)").bitcast(F32), 0.0)
         for a in range(QUARTERS):

@@ -52,7 +52,7 @@ def tile_canonglufeedforwardlayer_w_kernel(
     with ExitStack() as ctx:
         ctx.enter_context(tc.manual_schedule())
         keep = ctx.enter_context(tc.tile_pool(name="keep", bufs=1))
-        unit_pool = ctx.enter_context(tc.tile_pool(name="unit_pool", bufs=UNIT_BUFFERS))
+        unit_pool = ctx.enter_context(tc.tile_pool(name="unit_pool", bufs=UNIT_BUFFERS * (UNIT // GROUP)))
         work = ctx.enter_context(tc.tile_pool(name="work", bufs=2))
         psum = ctx.enter_context(tc.psum_pool(name="psum", bufs=1))
 
@@ -80,11 +80,12 @@ def tile_canonglufeedforwardlayer_w_kernel(
 
         def load_unit(index):
             rnd, branch = divmod(index, 2)
-            unit_words = unit_pool.tile([P, D_GROUPS, UNIT], U32, name="unit_words", align_bytes=DMA_ALIGN)
-            nc.sync.dma_start(
-                out=unit_words[:].bitcast(I32), in_=branch_words[branch][:, :, UNIT * rnd : UNIT * (rnd + 1)]
-            )
-            units[(rnd, branch)] = unit_words
+            for c in range((UNIT // GROUP) * rnd, (UNIT // GROUP) * (rnd + 1)):
+                unit_words = unit_pool.tile([P, D_GROUPS, GROUP], U32, name="unit_words", align_bytes=DMA_ALIGN)
+                nc.sync.dma_start(
+                    out=unit_words[:].bitcast(I32), in_=branch_words[branch][:, :, GROUP * c : GROUP * (c + 1)]
+                )
+                units[(c, branch)] = unit_words
 
         down_words = {}
         skipped = []
@@ -188,12 +189,11 @@ def tile_canonglufeedforwardlayer_w_kernel(
         h_grouped = {}
 
         def first_passes(c, branch):
-            rnd, part = divmod(c, UNIT // GROUP)
-            unit_words = units[(rnd, branch)]
+            unit_words = units[(c, branch)]
             planes = (gate_planes, up_planes)[branch]
             raw = psum.tile([P, QUARTERS, T], F32, name="raw", tag="raw", bufs=RAW_BANKS)
             for a in range(QUARTERS):
-                in_unit = GROUP * part + P * a
+                in_unit = P * a
                 in_branch = GROUP * c + P * a
                 for g in range(D_GROUPS):
                     nc.tensor.matmul_mx(

@@ -28,9 +28,13 @@ TILE_PLANES = 4
 PLANE_ROWS = 4
 LIVE_ROWS = TILE_PLANES * PLANE_ROWS
 CHANNEL_TILES = 2 * F // P
-UNIT = 2 * GROUP
-ROUNDS = F // UNIT
-UNIT_BUFFERS = 6
+JOBS = (
+    tuple((c, 0) for c in range(4))
+    + tuple((c, 1) for c in range(4))
+    + tuple((c0 + c, branch) for c0 in (4, 6) for branch in (0, 1) for c in (0, 1))
+)
+JOB_BUFFERS = 12
+GATE_ACT_BUFFERS = 4
 RAW_BANKS = 3
 DOWN_PIECES = tuple((c, 0, D) for c in range(F_GROUPS - 2)) + (
     (F_GROUPS - 2, 0, D // 2),
@@ -40,7 +44,7 @@ DOWN_PIECES = tuple((c, 0, D) for c in range(F_GROUPS - 2)) + (
     (F_GROUPS - 1, D // 2 + GROUP, GROUP),
 )
 QUADRANT_ORDER = (0, 2, 1, 3)
-SKIPS = 12
+SKIPS = 16
 DMA_ALIGN = 256
 FLOPS = 3 * 2 * T * D * F
 
@@ -52,7 +56,7 @@ def tile_canonglufeedforwardlayer_w_kernel(
     with ExitStack() as ctx:
         ctx.enter_context(tc.manual_schedule())
         keep = ctx.enter_context(tc.tile_pool(name="keep", bufs=1))
-        unit_pool = ctx.enter_context(tc.tile_pool(name="unit_pool", bufs=UNIT_BUFFERS * (UNIT // GROUP)))
+        unit_pool = ctx.enter_context(tc.tile_pool(name="unit_pool", bufs=JOB_BUFFERS))
         work = ctx.enter_context(tc.tile_pool(name="work", bufs=2))
         psum = ctx.enter_context(tc.psum_pool(name="psum", bufs=1))
 
@@ -78,14 +82,12 @@ def tile_canonglufeedforwardlayer_w_kernel(
         )
         units = {}
 
-        def load_unit(index):
-            rnd, branch = divmod(index, 2)
-            for c in range((UNIT // GROUP) * rnd, (UNIT // GROUP) * (rnd + 1)):
-                unit_words = unit_pool.tile([P, D_GROUPS, GROUP], U32, name="unit_words", align_bytes=DMA_ALIGN)
-                nc.sync.dma_start(
-                    out=unit_words[:].bitcast(I32), in_=branch_words[branch][:, :, GROUP * c : GROUP * (c + 1)]
-                )
-                units[(c, branch)] = unit_words
+        def load_job(c, branch):
+            unit_words = unit_pool.tile([P, D_GROUPS, GROUP], U32, name="unit_words", align_bytes=DMA_ALIGN)
+            nc.sync.dma_start(
+                out=unit_words[:].bitcast(I32), in_=branch_words[branch][:, :, GROUP * c : GROUP * (c + 1)]
+            )
+            units[(c, branch)] = unit_words
 
         down_words = {}
         skipped = []
@@ -119,22 +121,18 @@ def tile_canonglufeedforwardlayer_w_kernel(
                 for n in range(first // GROUP, (first + cols) // GROUP):
                     down_words[(c, n)] = words[:, GROUP * n - first : GROUP * (n + 1) - first]
 
-        for index in range(UNIT_BUFFERS):
-            load_unit(index)
+        for c, branch in JOBS[0:JOB_BUFFERS]:
+            load_job(c, branch)
 
         identity = keep.tile([P, P], F32, name="identity")
         make_identity(nc, identity[:])
-        for quad in range(P // QUADRANT):
-            nc.gpsimd.dma_start(
-                out=gate_planes[QUADRANT * quad : QUADRANT * quad + LIVE_ROWS, :].bitcast(F32),
-                in_=w_gate_scales[:, PLANE_ROWS * quad : PLANE_ROWS * (quad + 1), :].bitcast(F32),
-            )
-        for quad in QUADRANT_ORDER:
-            nc.gpsimd.dma_start(
-                out=up_planes[QUADRANT * quad : QUADRANT * quad + LIVE_ROWS, :].bitcast(F32),
-                in_=w_up_scales[:, PLANE_ROWS * quad : PLANE_ROWS * (quad + 1), :].bitcast(F32),
-            )
-            skip_four_engines(quad // 2)
+        for planes, scales in ((gate_planes, w_gate_scales), (up_planes, w_up_scales)):
+            for quad in QUADRANT_ORDER:
+                nc.gpsimd.dma_start(
+                    out=planes[QUADRANT * quad : QUADRANT * quad + LIVE_ROWS, :].bitcast(F32),
+                    in_=scales[:, PLANE_ROWS * quad : PLANE_ROWS * (quad + 1), :].bitcast(F32),
+                )
+                skip_four_engines(quad // 2)
         selectors = keep.tile([P, PACK, QUARTERS, P], BF16, name="selectors")
         nc.gpsimd.memset(selectors[:].rearrange("m j a p -> m (j a p)").bitcast(F32), 0.0)
         for a in range(QUARTERS):
@@ -236,7 +234,7 @@ def tile_canonglufeedforwardlayer_w_kernel(
                     )
 
         def gate_silu(c):
-            gate_act = work.tile([P, QUARTERS, T], F32, name="gate_act")
+            gate_act = work.tile([P, QUARTERS, T], F32, name="gate_act", bufs=GATE_ACT_BUFFERS)
             nc.scalar.activation(out=gate_act[:], in_=convolved[(c, 0)][:], func=ACT.Silu)
             gate_acts[c] = gate_act
 
@@ -288,38 +286,25 @@ def tile_canonglufeedforwardlayer_w_kernel(
                     stop=(c == F_GROUPS - 1),
                 )
 
-        for rnd in range(ROUNDS):
-            c0 = 2 * rnd
-            c1 = c0 + 1
-            first_passes(c0, 0)
-            present_term(c0, 0)
-            if rnd > 0:
-                move_rows(c0 - 2)
-                lay_words(c0 - 2)
-            first_passes(c1, 0)
-            present_term(c1, 0)
-            older_terms(c0, 0)
-            if rnd > 0:
-                quantise_h(c0 - 2)
-            gate_silu(c0)
-            if rnd > 0:
-                move_rows(c0 - 1)
-                lay_words(c0 - 1)
-            older_terms(c1, 0)
-            if rnd > 0:
-                quantise_h(c0 - 1)
-            first_passes(c0, 1)
-            present_term(c0, 1)
-            gate_silu(c1)
-            first_passes(c1, 1)
-            present_term(c1, 1)
-            older_terms(c0, 1)
-            up_times_gate(c0)
-            older_terms(c1, 1)
-            up_times_gate(c1)
-            if rnd == 0:
-                load_unit(UNIT_BUFFERS)
-                load_unit(UNIT_BUFFERS + 1)
+        made = {}
+        for step, (c, branch) in enumerate(JOBS):
+            first_passes(c, branch)
+            present_term(c, branch)
+            if step > 0 and JOBS[step - 1][1] == 0:
+                gate_silu(JOBS[step - 1][0])
+            moved = made.get(step - 2)
+            if moved is not None:
+                move_rows(moved)
+                lay_words(moved)
+            older_terms(c, branch)
+            if branch == 1:
+                up_times_gate(c)
+                made[step] = c
+            if moved is not None:
+                quantise_h(moved)
+            if step == len(JOBS) - JOB_BUFFERS - 1:
+                for late_c, late_branch in JOBS[JOB_BUFFERS:]:
+                    load_job(late_c, late_branch)
                 load_down_words()
         for piece in DOWN_PIECES[0:4]:
             down_passes(piece)

from contextlib import ExitStack

import concourse.mybir as mybir
from concourse.masks import make_identity

F32 = mybir.dt.float32
BF16 = mybir.dt.bfloat16
I32 = mybir.dt.int32
U32 = mybir.dt.uint32
U8 = mybir.dt.uint8
FP8X4 = mybir.dt.float8_e4m3fn_x4
ALU = mybir.AluOpType
ACT = mybir.ActivationFunctionType

P = 128
T = 128
D = 2048
F = 4096
TAPS = 4
PACK = 4
GROUP = P * PACK
D_GROUPS = D // GROUP
F_GROUPS = F // GROUP
OUT_BANKS = D // GROUP
QUARTERS = GROUP // P
QUADRANT = 32
TILE_PLANES = 4
PLANE_ROWS = 4
LIVE_ROWS = TILE_PLANES * PLANE_ROWS
CHANNEL_TILES = 2 * F // P
JOBS = (
    tuple((c, 0) for c in range(4))
    + tuple((c, 1) for c in range(4))
    + tuple((c0 + c, branch) for c0 in (4, 6) for branch in (0, 1) for c in (0, 1))
)
JOB_BUFFERS = 12
GATE_ACT_BUFFERS = 4
RAW_BANKS = 3
DOWN_PIECES = tuple((c, 0, D) for c in range(F_GROUPS - 2)) + (
    (F_GROUPS - 2, 0, D // 2),
    (F_GROUPS - 1, 0, D // 2),
    (F_GROUPS - 2, D // 2, D // 2),
    (F_GROUPS - 1, D // 2, GROUP),
    (F_GROUPS - 1, D // 2 + GROUP, GROUP),
)
QUADRANT_ORDER = (0, 2, 1, 3)
SKIPS = 16
DMA_ALIGN = 256
FLOPS = 3 * 2 * T * D * F


def tile_canonglufeedforwardlayer_w_kernel(
    tc, x, w_gate_words, w_gate_scales, w_up_words, w_up_scales, w_down_words, w_down_scales, conv_w, out
):
    nc = tc.nc
    with ExitStack() as ctx:
        ctx.enter_context(tc.manual_schedule())
        keep = ctx.enter_context(tc.tile_pool(name="keep", bufs=1))
        unit_pool = ctx.enter_context(tc.tile_pool(name="unit_pool", bufs=JOB_BUFFERS))
        work = ctx.enter_context(tc.tile_pool(name="work", bufs=2))
        psum = ctx.enter_context(tc.psum_pool(name="psum", bufs=1))

        gate_planes = keep.tile([P, F], U8, name="gate_planes", align_bytes=DMA_ALIGN)
        up_planes = keep.tile([P, F], U8, name="up_planes", align_bytes=DMA_ALIGN)
        down_planes = keep.tile([P, F_GROUPS // TILE_PLANES, D], U8, name="down_planes", align_bytes=DMA_ALIGN)
        conv_rows = keep.tile([P, P * TAPS], BF16, name="conv_rows")
        scratch = keep.tile([P, 8], F32, name="scratch")
        nc.vector.memset(gate_planes[:].bitcast(I32), 0)
        nc.vector.memset(conv_rows[:].bitcast(I32), 0)
        nc.vector.memset(scratch[:], 0.0)
        nc.vector.memset(up_planes[:].bitcast(I32), 0)
        nc.vector.memset(down_planes[:].rearrange("p r n -> p (r n)").bitcast(I32), 0)

        x_rows = keep.tile([P, D], BF16, name="x_rows", align_bytes=DMA_ALIGN)
        nc.sync.dma_start(out=x_rows[:], in_=x.rearrange("b t d -> (b t) d"))
        nc.scalar.dma_start(out=conv_rows[0:CHANNEL_TILES, :], in_=conv_w.rearrange("(i m) w -> i (m w)", m=P))
        nc.scalar.activation(out=scratch[:, 4:8], in_=scratch[:, 0:4], func=ACT.Silu)

        branch_words = (
            w_gate_words.rearrange("g p n j -> p g (n j)").bitcast(I32),
            w_up_words.rearrange("g p n j -> p g (n j)").bitcast(I32),
        )
        units = {}

        def load_job(c, branch):
            unit_words = unit_pool.tile([P, D_GROUPS, GROUP], U32, name="unit_words", align_bytes=DMA_ALIGN)
            nc.sync.dma_start(
                out=unit_words[:].bitcast(I32), in_=branch_words[branch][:, :, GROUP * c : GROUP * (c + 1)]
            )
            units[(c, branch)] = unit_words

        down_words = {}
        skipped = []
        skip_bytes = keep.tile([P, SKIPS, 16], F32, name="skip_bytes")

        def skip_four_engines(half):
            first = (P // 2) * half + LIVE_ROWS
            nc.gpsimd.dma_start(
                out=skip_bytes[first : first + LIVE_ROWS, len(skipped), :],
                in_=w_gate_scales[:, 0:PLANE_ROWS, 0:64].bitcast(F32),
            )
            skipped.append(half)

        def load_down_planes(col_range):
            for quad in QUADRANT_ORDER:
                nc.gpsimd.dma_start(
                    out=down_planes[QUADRANT * quad : QUADRANT * quad + LIVE_ROWS, col_range, :].bitcast(F32),
                    in_=w_down_scales[
                        TILE_PLANES * col_range : TILE_PLANES * (col_range + 1),
                        PLANE_ROWS * quad : PLANE_ROWS * (quad + 1),
                        :,
                    ].bitcast(F32),
                )
                skip_four_engines(quad // 2)

        def load_down_words():
            for c, first, cols in DOWN_PIECES:
                source = w_down_words[c].rearrange("p n j -> p (n j)").bitcast(I32)
                words = keep.tile([P, cols], U32, name="down_words_%d_%d" % (c, first), align_bytes=DMA_ALIGN)
                nc.sync.dma_start(out=words[:].bitcast(I32), in_=source[:, first : first + cols])
                for n in range(first // GROUP, (first + cols) // GROUP):
                    down_words[(c, n)] = words[:, GROUP * n - first : GROUP * (n + 1) - first]

        for c, branch in JOBS[0:JOB_BUFFERS]:
            load_job(c, branch)

        identity = keep.tile([P, P], F32, name="identity")
        make_identity(nc, identity[:])
        for planes, scales in ((gate_planes, w_gate_scales), (up_planes, w_up_scales)):
            for quad in QUADRANT_ORDER:
                nc.gpsimd.dma_start(
                    out=planes[QUADRANT * quad : QUADRANT * quad + LIVE_ROWS, :].bitcast(F32),
                    in_=scales[:, PLANE_ROWS * quad : PLANE_ROWS * (quad + 1), :].bitcast(F32),
                )
                skip_four_engines(quad // 2)
        selectors = keep.tile([P, PACK, QUARTERS, P], BF16, name="selectors")
        nc.gpsimd.memset(selectors[:].rearrange("m j a p -> m (j a p)").bitcast(F32), 0.0)
        for a in range(QUARTERS):
            nc.gpsimd.tensor_copy(
                out=selectors[:, :, a, (P // PACK) * a : (P // PACK) * (a + 1)],
                in_=identity[:].rearrange("m (r j) -> m j r", j=PACK),
            )
        for col_range in range(F_GROUPS // TILE_PLANES):
            load_down_planes(col_range)

        conv_f32 = keep.tile([P, TAPS, P], F32, name="conv_f32")
        nc.vector.tensor_copy(out=conv_f32[:], in_=conv_rows[:].rearrange("i (m w) -> i w m", w=TAPS))

        x_grouped = keep.tile([P, D], BF16, name="x_grouped", align_bytes=64)
        x_words = keep.tile([P, D_GROUPS, T], U32, name="x_words", align_bytes=64)
        x_planes = keep.tile([P, D_GROUPS, T], U8, name="x_planes", align_bytes=64)
        x_as_f32 = x_rows[:].bitcast(F32)
        x_grouped_as_f32 = x_grouped[:].bitcast(F32).rearrange("p (g t u) -> p g t u", g=D_GROUPS, t=T, u=2)
        for half in range(2):
            x_t = psum.tile([P, 4, P], F32, name="x_t", tag="raw", bufs=RAW_BANKS)
            for g in (2 * half, 2 * half + 1):
                for u in range(2):
                    nc.tensor.transpose(
                        x_t[:, 2 * (g % 2) + u, :],
                        x_as_f32[:, (GROUP // 2) * g + u : (GROUP // 2) * (g + 1) : 2],
                        identity[:],
                    )
            side_by_side = x_t[:].rearrange("p (g u) t -> p g t u", u=2)
            if half == 0:
                nc.vector.tensor_copy(out=x_grouped_as_f32[:, 0:2], in_=side_by_side)
            else:
                nc.scalar.copy(out=x_grouped_as_f32[:, 2:4], in_=side_by_side)
        conv_t = psum.tile([P, TAPS, P], F32, name="conv_t", tag="raw", bufs=RAW_BANKS)
        for tap in range(TAPS):
            nc.tensor.transpose(conv_t[:, tap, :], conv_f32[:, tap, :], identity[:])
        nc.vector.quantize_mx(
            out=x_words[:].rearrange("p g t -> p (g t)").bitcast(FP8X4),
            scales=x_planes[:].rearrange("p g t -> p (g t)"),
            in_=x_grouped[:],
        )
        taps = keep.tile([P, TAPS, CHANNEL_TILES], F32, name="taps")
        nc.vector.tensor_copy(out=taps[:], in_=conv_t[:, :, 0:CHANNEL_TILES])
        nc.vector.tensor_scalar_add(out=taps[:, TAPS - 1, :], in0=taps[:, TAPS - 1, :], scalar1=1.0)

        h_words = keep.tile([P, F_GROUPS, T], U32, name="h_words", align_bytes=64)
        h_planes = keep.tile([P, F_GROUPS, T], U8, name="h_planes", align_bytes=64)
        raws = {}
        convolved = {}
        gate_acts = {}
        h_by_channel = {}
        h_moved = {}
        h_grouped = {}

        def first_passes(c, branch):
            unit_words = units[(c, branch)]
            planes = (gate_planes, up_planes)[branch]
            raw = psum.tile([P, QUARTERS, T], F32, name="raw", tag="raw", bufs=RAW_BANKS)
            for a in range(QUARTERS):
                in_unit = P * a
                in_branch = GROUP * c + P * a
                for g in range(D_GROUPS):
                    nc.tensor.matmul_mx(
                        out=raw[:, a, :],
                        lhsT=unit_words[:, g, in_unit : in_unit + P].bitcast(FP8X4),
                        lhsT_scale=planes[PLANE_ROWS * g : P, in_branch : in_branch + P],
                        rhs=x_words[:, g, :].bitcast(FP8X4),
                        rhs_scale=x_planes[:, g, :],
                        start=(g == 0),
                        stop=(g == D_GROUPS - 1),
                    )
            raws[(c, branch)] = raw

        def present_term(c, branch):
            raw = raws[(c, branch)]
            conv = work.tile([P, QUARTERS, T], F32, name="conv%d" % branch)
            tile0 = (F // P) * branch + QUARTERS * c
            for a in range(QUARTERS):
                nc.scalar.activation(
                    out=conv[:, a, :],
                    in_=raw[:, a, :],
                    func=ACT.Copy,
                    scale=taps[:, TAPS - 1, tile0 + a : tile0 + a + 1],
                )
            convolved[(c, branch)] = conv

        def older_terms(c, branch):
            raw = raws[(c, branch)]
            conv = convolved[(c, branch)]
            tile0 = (F // P) * branch + QUARTERS * c
            for s in range(1, TAPS):
                for a in reversed(range(QUARTERS)):
                    nc.vector.scalar_tensor_tensor(
                        out=conv[:, a, s:T],
                        in0=raw[:, a, 0 : T - s],
                        scalar=taps[:, TAPS - 1 - s, tile0 + a : tile0 + a + 1],
                        in1=conv[:, a, s:T],
                        op0=ALU.mult,
                        op1=ALU.add,
                    )

        def gate_silu(c):
            gate_act = work.tile([P, QUARTERS, T], F32, name="gate_act", bufs=GATE_ACT_BUFFERS)
            nc.scalar.activation(out=gate_act[:], in_=convolved[(c, 0)][:], func=ACT.Silu)
            gate_acts[c] = gate_act

        def up_times_gate(c):
            h_channel = work.tile([P, QUARTERS, T], BF16, name="h_channel")
            nc.vector.tensor_tensor(out=h_channel[:], in0=convolved[(c, 1)][:], in1=gate_acts[c][:], op=ALU.mult)
            h_by_channel[c] = h_channel

        def move_rows(c):
            h_rows = psum.tile([P, PACK, T], F32, name="h_rows", tag="h_rows", bufs=1)
            for j in range(PACK):
                for a in range(QUARTERS):
                    nc.tensor.matmul(
                        out=h_rows[:, j, :],
                        lhsT=selectors[:, j, a, :],
                        rhs=h_by_channel[c][:, a, :],
                        start=(a == 0),
                        stop=(a == QUARTERS - 1),
                    )
            h_moved[c] = h_rows

        def lay_words(c):
            h_side_by_side = work.tile([P, T, PACK], BF16, name="h_side_by_side", align_bytes=64)
            nc.scalar.copy(out=h_side_by_side[:], in_=h_moved[c][:].rearrange("p j t -> p t j"))
            h_grouped[c] = h_side_by_side

        def quantise_h(c):
            nc.vector.quantize_mx(
                out=h_words[:, c, :].bitcast(FP8X4),
                scales=h_planes[:, c, :],
                in_=h_grouped[c][:].rearrange("p t j -> p (t j)"),
            )

        out_banks = []
        for n in range(OUT_BANKS):
            out_bank = psum.tile([P, GROUP], F32, name="out_bank%d" % n, tag="out_bank%d" % n, bufs=1)
            out_banks.append(out_bank)

        def down_passes(piece):
            c, first, cols = piece
            for n in range(first // GROUP, (first + cols) // GROUP):
                nc.tensor.matmul_mx(
                    out=out_banks[n][:],
                    lhsT=h_words[:, c, :].bitcast(FP8X4),
                    lhsT_scale=h_planes[:, c, :],
                    rhs=down_words[(c, n)].bitcast(FP8X4),
                    rhs_scale=down_planes[PLANE_ROWS * (c % TILE_PLANES) : P, c // TILE_PLANES, GROUP * n : GROUP * (n + 1)],
                    start=(c == 0),
                    stop=(c == F_GROUPS - 1),
                )

        made = {}
        for step, (c, branch) in enumerate(JOBS):
            first_passes(c, branch)
            present_term(c, branch)
            if step > 0 and JOBS[step - 1][1] == 0:
                gate_silu(JOBS[step - 1][0])
            moved = made.get(step - 2)
            if moved is not None:
                move_rows(moved)
                lay_words(moved)
            older_terms(c, branch)
            if branch == 1:
                up_times_gate(c)
                made[step] = c
            if moved is not None:
                quantise_h(moved)
            if step == len(JOBS) - JOB_BUFFERS - 1:
                for late_c, late_branch in JOBS[JOB_BUFFERS:]:
                    load_job(late_c, late_branch)
                load_down_words()
        for piece in DOWN_PIECES[0:4]:
            down_passes(piece)
        move_rows(F_GROUPS - 2)
        lay_words(F_GROUPS - 2)
        quantise_h(F_GROUPS - 2)
        down_passes(DOWN_PIECES[4])
        move_rows(F_GROUPS - 1)
        lay_words(F_GROUPS - 1)
        quantise_h(F_GROUPS - 1)
        for piece in DOWN_PIECES[5:]:
            down_passes(piece)

        out_rows = keep.tile([P, D], F32, name="out_rows", align_bytes=DMA_ALIGN)
        out_flat = out.rearrange("b t d -> (b t) d")
        for c, first, cols in DOWN_PIECES:
            if c == F_GROUPS - 1:
                for n in range(first // GROUP, (first + cols) // GROUP):
                    if n % 2 == 0:
                        nc.vector.tensor_copy(out=out_rows[:, GROUP * n : GROUP * (n + 1)], in_=out_banks[n][:])
                    else:
                        nc.scalar.copy(out=out_rows[:, GROUP * n : GROUP * (n + 1)], in_=out_banks[n][:])
                nc.sync.dma_start(out=out_flat[:, first : first + cols], in_=out_rows[:, first : first + cols])
